import numpy as np
import ml_dtypes


def mxq(x, axis, fmt="e4m3"):
    dtype, down = {"e4m3": (ml_dtypes.float8_e4m3fn, 7), "e5m2": (ml_dtypes.float8_e5m2, 14)}[fmt]
    v = np.moveaxis(np.asarray(x, np.float32).astype(ml_dtypes.bfloat16).astype(np.float64), axis, -1)
    blocks = v.reshape(v.shape[:-1] + (-1, 32))
    amax = np.abs(blocks).max(-1, keepdims=True)
    byte = np.maximum(np.where(amax > 0, np.frexp(amax)[1] - 1 + 127, 0) - down, 1)
    scale = np.exp2(byte - 127.0)
    codes = (blocks / scale).astype(np.float32).astype(dtype).astype(np.float64)
    return np.moveaxis((codes * scale).reshape(v.shape), -1, axis)


WIDE = False


def mx_kscale(k):
    if not WIDE:
        return np.ones(k)
    levels = np.array([10, -10, 5, -5, 0])
    if k % 512:
        return np.exp2(np.random.permutation(np.resize(levels, k // 32))).repeat(32)
    a = np.empty((k // 512, 16))
    for p in range(k // 512):
        a[p, :8] = np.random.permutation(np.resize(levels, 8))
        for g in range(8):
            far = levels[np.abs(levels - a[p, g]) >= 10]
            a[p, g + 8] = far[np.random.randint(len(far))]
    return np.exp2(a.ravel()).repeat(32)


BF16 = ml_dtypes.bfloat16


def bf(x):
    return np.asarray(x, np.float32).astype(BF16)


def f64(x):
    return np.asarray(x).astype(np.float64)


B, S, E, H = 2, 1024, 1024, 4
D = E // H
LN_EPS = 1e-6


def setup_inputs():
    s = mx_kscale(E)
    return {"h_attn": bf(np.random.standard_normal((B, H, S, D)) * 0.4 * s.reshape(H, 1, D)),
            "x": bf(np.random.standard_normal((B, S, E))),
            "out_w": bf(np.random.standard_normal((E, E)) * 2.0 / np.sqrt(E) / s[:, None]),
            "ln_gamma": bf(1.0 + 0.1 * np.random.standard_normal(E)),
            "ln_beta": bf(0.1 * np.random.standard_normal(E))}


def core(h_attn, x, out_w, ln_gamma, ln_beta):
    merged = f64(h_attn).transpose(0, 2, 1, 3).reshape(B, S, E)
    out = mxq(merged, 2, "e4m3") @ mxq(f64(out_w), 0, "e4m3")
    y = out + f64(x)
    mean = y.mean(-1, keepdims=True)
    var = np.square(y - mean).mean(-1, keepdims=True)
    return (y - mean) / np.sqrt(var + LN_EPS) * f64(ln_gamma) + f64(ln_beta)


def e4m3fn_bytes(y):
    return np.clip(np.asarray(y, np.float64), -448.0, 448.0).astype(np.float32).astype(ml_dtypes.float8_e4m3fn).view(np.uint8)


def reference(h_attn, x, out_w, ln_gamma, ln_beta):
    out = core(h_attn, x, out_w, ln_gamma, ln_beta)
    s = np.max(np.abs(out), axis=-1, keepdims=True) / 448.0
    return out, e4m3fn_bytes(out / s)

@@ -1,0 +1,339 @@
+from contextlib import ExitStack
+
+import concourse.mybir as mybir
+from concourse.masks import make_identity
+
+B, H, S, D = 2, 4, 1024, 256
+E = H * D
+LN_EPS = 1e-6
+FLOPS = 2 * B * S * E * E
+
+F32 = mybir.dt.float32
+BF16 = mybir.dt.bfloat16
+U32 = mybir.dt.uint32
+U8 = mybir.dt.uint8
+FP8X4 = mybir.dt.float8_e4m3fn_x4
+FP8 = mybir.dt.float8_e4m3fn
+ALU = mybir.AluOpType
+ACT = mybir.ActivationFunctionType
+AX = mybir.AxisListType
+
+P = 128
+J = 2
+NG = B * S // (P * J)
+NT = NG * J
+NB = 512
+NC = E // NB
+NP = E // 512
+NV = 336
+FC = 512
+LAST_SPLIT = 352
+
+
+def tile_selfattention_pa_kernel(tc, h_attn, x, out_w, ln_gamma, ln_beta, out_0, out_1):
+    nc = tc.nc
+    hv = h_attn.rearrange("b h (q p j) d -> b q j p h d", p=P, j=J)
+    xv = x.rearrange("b (q p j) n -> b q j p n", p=P, j=J)
+    o0v = out_0.rearrange("b (q p j) n -> b q j p n", p=P, j=J)
+    o1v = out_1.rearrange("b (q p j) n -> b q p j n", p=P, j=J)
+    wv = out_w.rearrange("(g p t) n -> g p t n", p=P, t=4)
+    QB = NG // B
+
+    with ExitStack() as ctx:
+        const = ctx.enter_context(tc.tile_pool(name="const", bufs=1))
+        inp = ctx.enter_context(tc.tile_pool(name="inp", bufs=1))
+        mxp = ctx.enter_context(tc.tile_pool(name="mxp", bufs=3))
+        work = ctx.enter_context(tc.tile_pool(name="work", bufs=3))
+        outp = ctx.enter_context(tc.tile_pool(name="outp", bufs=7))
+        stat = ctx.enter_context(tc.tile_pool(name="stat", bufs=4))
+        ps_acc = ctx.enter_context(tc.psum_pool(name="ps_acc", bufs=4))
+        ps_xt = ctx.enter_context(tc.psum_pool(name="ps_xt", bufs=2))
+        ps_c = ctx.enter_context(tc.psum_pool(name="ps_c", bufs=1))
+        ctx.enter_context(tc.manual_schedule())
+
+        ident = const.tile([P, P], F32, name="ident")
+        make_identity(nc, ident[:])
+        crow = const.tile([P, 2 * E], BF16, name="crow")
+        nc.vector.memset(crow[:], 0.0)
+        eps_t = const.tile([P, 1], F32, name="eps_t")
+        nc.vector.memset(eps_t[:], LN_EPS)
+        zero_t = const.tile([P, 1], F32, name="zero_t")
+        nc.vector.memset(zero_t[:], 0.0)
+        ones = const.tile([P, P], BF16, name="ones")
+        nc.vector.memset(ones[:], 1.0)
+        warm = const.tile([P, 1], F32, name="warm")
+        nc.scalar.dma_start(out=crow[0:1, 0:E], in_=ln_gamma.rearrange("(o n) -> o n", o=1))
+        nc.scalar.dma_start(out=crow[0:1, E:2 * E], in_=ln_beta.rearrange("(o n) -> o n", o=1))
+        nc.scalar.activation(out=warm[:], in_=eps_t[:], func=ACT.Abs_reciprocal_sqrt)
+
+        hs = {}
+        xs = {}
+        wraw = {}
+
+        def load_h(i):
+            gi, j = divmod(i, J)
+            if j == 0:
+                hs[gi] = inp.tile([P, J, E], BF16, name="hs%d" % gi)
+            nc.sync.dma_start(
+                out=hs[gi][:, j, :].rearrange("p (h d) -> p h d", h=H),
+                in_=hv[gi // QB, gi % QB, j],
+            )
+
+        def load_x(i):
+            gi, j = divmod(i, J)
+            if j == 0:
+                xs[gi] = inp.tile([P, J, E], BF16, name="xs%d" % gi)
+            nc.sync.dma_start(out=xs[gi][:, j, :], in_=xv[gi // QB, gi % QB, j])
+
+        def load_w(c, g):
+            if g == 0:
+                wraw[c] = inp.tile([P, NP, 4, NB], BF16, name="wraw%d" % c)
+            nc.sync.dma_start(out=wraw[c][:, g, :, :], in_=wv[g, :, :, c * NB:(c + 1) * NB])
+
+        load_w(0, 0)
+        load_w(0, 1)
+        load_h(0)
+        load_x(0)
+        load_w(1, 0)
+        load_w(1, 1)
+        load_h(1)
+        for i in range(2, NT):
+            load_h(i)
+            load_x(i - 1)
+        load_x(NT - 1)
+
+        gt = const.tile([P, E], F32, name="gt")
+        bt = {}
+
+        def spread_gamma_beta():
+            for c in range(NC):
+                gp = ps_xt.tile([P, NB], F32, name="gp", tag="xt")
+                nc.tensor.matmul(gp[:], lhsT=ones[:], rhs=crow[:, c * NB:(c + 1) * NB], start=True, stop=True)
+                nc.scalar.copy(out=gt[:, c * NB:(c + 1) * NB], in_=gp[:])
+                bt[c] = ps_c.tile([P, NB], F32, name="bt%d" % c)
+                nc.tensor.matmul(
+                    bt[c][:], lhsT=ones[:], rhs=crow[:, E + c * NB:E + (c + 1) * NB], start=True, stop=True
+                )
+
+        wgr = {}
+        wc = {}
+        ws = {}
+
+        def w_interleave(c, g):
+            if g == 0:
+                wgr[c] = inp.tile([P, NP, NB, 4], BF16, name="wgr%d" % c, align_bytes=64)
+            nc.vector.tensor_copy(out=wgr[c][:, g, 0:NV, :], in_=wraw[c][:, g, :, 0:NV].rearrange("p t n -> p n t"))
+            nc.scalar.copy(out=wgr[c][:, g, NV:NB, :], in_=wraw[c][:, g, :, NV:NB].rearrange("p t n -> p n t"))
+
+        def w_quant(c, g):
+            if g == 0:
+                wc[c] = inp.tile([P, NP, NB], U32, name="wc%d" % c, align_bytes=64)
+                ws[c] = inp.tile([P, NP, NB], U8, name="ws%d" % c, align_bytes=64)
+            nc.vector.quantize_mx(
+                out=wc[c][:, g, :].bitcast(FP8X4),
+                scales=ws[c][:, g, :],
+                in_=wgr[c][:, g, :, :].rearrange("p n t -> p (n t)"),
+            )
+
+        mg = {}
+        mc = {}
+        ms = {}
+        acc = {}
+        yt = {}
+        yc = {}
+        ut = {}
+        ot = {}
+        o8 = {}
+        vst = {}
+        sst = {}
+
+        xts = {}
+
+        def front_pe(i):
+            gi, j = divmod(i, J)
+            words = hs[gi][:, j, :].bitcast(F32)
+            xts[i] = ps_xt.tile([P, NP, 2, P], F32, name="xt", tag="xt")
+            for g in range(NP):
+                for u in range(2):
+                    nc.tensor.transpose(xts[i][:, g, u, :], words[:, 256 * g + u:256 * (g + 1):2], ident[:])
+
+        def front_s(i):
+            mg[i] = mxp.tile([P, NP, P, 4], BF16, name="mg", align_bytes=64)
+            nc.scalar.copy(out=mg[i][:].bitcast(F32), in_=xts[i][:].rearrange("p g u r -> p g r u"))
+
+        def quant(i):
+            mc[i] = mxp.tile([P, NP * P], U32, name="mc", align_bytes=64)
+            ms[i] = mxp.tile([P, NP * P], U8, name="ms", align_bytes=64)
+            nc.vector.quantize_mx(
+                out=mc[i][:].bitcast(FP8X4),
+                scales=ms[i][:],
+                in_=mg[i][:].rearrange("p g r t -> p (g r t)"),
+            )
+
+        def mmc(i, c):
+            acc[i, c] = ps_acc.tile([P, NB], F32, name="acc")
+            for g in range(NP):
+                nc.tensor.matmul_mx(
+                    out=acc[i, c][:],
+                    lhsT=mc[i][:, g * P:(g + 1) * P].bitcast(FP8X4),
+                    lhsT_scale=ms[i][:, g * P:(g + 1) * P],
+                    rhs=wc[c][:, g, :].bitcast(FP8X4),
+                    rhs_scale=ws[c][:, g, :],
+                    start=(g == 0),
+                    stop=(g == NP - 1),
+                )
+
+        def p1c(i, c):
+            gi, j = divmod(i, J)
+            if c == 0:
+                if j == 0:
+                    vst[gi] = stat.tile([P, 8], F32, name="vst")
+                    sst[gi] = stat.tile([P, 16], F32, name="sst")
+                yt[i] = work.tile([P, E], F32, name="yt")
+            nc.vector.scalar_tensor_tensor(
+                out=yt[i][:, c * NB:(c + 1) * NB],
+                in0=xs[gi][:, j, c * NB:(c + 1) * NB],
+                scalar=1.0,
+                in1=acc[i, c][:],
+                op0=ALU.mult,
+                op1=ALU.add,
+                accum_out=vst[gi][:, 2 * j + c:2 * j + c + 1],
+            )
+
+        def mid(i):
+            gi, j = divmod(i, J)
+            negmean = sst[gi][:, 6 + j:7 + j]
+            nc.scalar.activation(
+                out=sst[gi][:, 8 + 2 * j:10 + 2 * j],
+                in_=vst[gi][:, 2 * j:2 * j + 2],
+                func=ACT.Copy,
+                scale=-1.0 / E,
+                accum_out=negmean,
+            )
+            yc[i] = work.tile([P, E], F32, name="yc")
+            ut[i] = work.tile([P, E], F32, name="ut", bufs=4)
+            junk = work.tile([P, E], BF16, name="junk", bufs=2)
+            nc.scalar.activation(
+                out=yc[i][:, 0:FC], in_=yt[i][:, 0:FC], func=ACT.Identity, bias=negmean, scale=1.0
+            )
+            nc.gpsimd.tensor_scalar(
+                out=yc[i][:, FC:E], in0=yt[i][:, FC:E], scalar1=negmean, scalar2=1.0, op0=ALU.add, op1=ALU.mult
+            )
+            nc.gpsimd.tensor_tensor(out=ut[i][:], in0=yc[i][:], in1=gt[:], op=ALU.mult)
+            nc.scalar.activation(
+                out=junk[:], in_=yt[i][:], func=ACT.Square, bias=negmean, scale=1.0, accum_out=sst[gi][:, j:j + 1]
+            )
+            nc.scalar.activation(
+                out=sst[gi][:, 2 + j:3 + j],
+                in_=sst[gi][:, j:j + 1],
+                func=ACT.Abs_reciprocal_sqrt,
+                bias=eps_t[:, 0:1],
+                scale=1.0 / E,
+            )
+
+        def fin(i):
+            gi, j = divmod(i, J)
+            ot[i] = outp.tile([P, E], F32, name="ot")
+            for c in range(NC):
+                nc.vector.scalar_tensor_tensor(
+                    out=ot[i][:, c * NB:(c + 1) * NB],
+                    in0=ut[i][:, c * NB:(c + 1) * NB],
+                    scalar=sst[gi][:, 2 + j:3 + j],
+                    in1=bt[c][:],
+                    op0=ALU.mult,
+                    op1=ALU.add,
+                )
+            nc.sync.dma_start(out=o0v[gi // QB, gi % QB, j], in_=ot[i][:])
+
+        def amax(i):
+            gi, j = divmod(i, J)
+            nc.vector.tensor_reduce(
+                out=vst[gi][:, 4 + j:5 + j], in_=ot[i][:], axis=AX.X, op=ALU.max, apply_absolute_value=True
+            )
+
+        def recip(gi, j0, j1):
+            nc.vector.reciprocal(out=vst[gi][:, 6 + j0:6 + j1], in_=vst[gi][:, 4 + j0:4 + j1])
+
+        def factor(gi, j0, j1):
+            nc.scalar.activation(
+                out=sst[gi][:, 4 + j0:4 + j1], in_=vst[gi][:, 6 + j0:6 + j1], func=ACT.Copy, scale=448.0
+            )
+
+        def cast(gi, j, split):
+            if j == 0:
+                o8[gi] = outp.tile([P, J, E], FP8, name="o8", bufs=3)
+            nc.scalar.activation(
+                out=o8[gi][:, j, 0:split],
+                in_=ot[gi * J + j][:, 0:split],
+                func=ACT.Identity,
+                scale=sst[gi][:, 4 + j:5 + j],
+                bias=zero_t[:, 0:1],
+                saturate=False,
+            )
+            if split < E:
+                nc.vector.tensor_scalar(
+                    out=o8[gi][:, j, split:E],
+                    in0=ot[gi * J + j][:, split:E],
+                    scalar1=sst[gi][:, 4 + j:5 + j],
+                    scalar2=None,
+                    op0=ALU.mult,
+                    saturate=False,
+                )
+            if j == J - 1:
+                nc.sync.dma_start(out=o1v[gi // QB, gi % QB], in_=o8[gi][:].bitcast(U8))
+
+        w_interleave(0, 0)
+        w_interleave(0, 1)
+        front_pe(0)
+        front_s(0)
+        w_quant(0, 0)
+        w_quant(0, 1)
+        quant(0)
+        mmc(0, 0)
+        w_interleave(1, 0)
+        p1c(0, 0)
+        w_interleave(1, 1)
+        front_pe(1)
+        front_s(1)
+        front_pe(2)
+        front_s(2)
+        spread_gamma_beta()
+        w_quant(1, 0)
+        w_quant(1, 1)
+        mmc(0, 1)
+        quant(1)
+        for t in range(NT + 3):
+            if t + 1 < NT:
+                mmc(t + 1, 0)
+                mmc(t + 1, 1)
+            if t + 3 < NT:
+                front_pe(t + 3)
+            if t < NT:
+                if t > 0:
+                    p1c(t, 0)
+                p1c(t, 1)
+            full = t >= 5 and (t - 5) % J == 0 and (t - 5) // J <= NG - 2
+            if full:
+                recip((t - 5) // J, 0, J)
+            if t + 2 < NT:
+                quant(t + 2)
+            if 0 <= t - 3 < NT:
+                amax(t - 3)
+            if t - 3 >= NT - J:
+                recip(NG - 1, (t - 3) % J, (t - 3) % J + 1)
+            if t < NT:
+                mid(t)
+            if t + 3 < NT:
+                front_s(t + 3)
+            if 0 <= t - 2 < NT:
+                fin(t - 2)
+            if full:
+                factor((t - 5) // J, 0, J)
+                cast((t - 5) // J, 0, E)
+            if t >= 6 and (t - 6) % J == 0 and (t - 6) // J <= NG - 3:
+                cast((t - 6) // J, 1, E)
+            if t == NT + 1:
+                cast(NG - 2, 1, E)
+            if t - 3 >= NT - J:
+                factor(NG - 1, (t - 3) % J, (t - 3) % J + 1)
+                cast(NG - 1, (t - 3) % J, E if t - 3 < NT - 1 else LAST_SPLIT)

@@ -26,7 +26,7 @@ NB = 512
 NC = E // NB
 NP = E // 512
 NV = 336
-FC = 512
+FC = 320
 LAST_SPLIT = 352
 
 

@@ -102,7 +102,7 @@ def tile_selfattention_pa_kernel(tc, h_attn, x, out_w, ln_gamma, ln_beta, out_0,
             load_x(i - 1)
         load_x(NT - 1)
 
-        gt = const.tile([P, E], F32, name="gt")
+        gt = const.tile([P, E], BF16, name="gt")
         bt = {}
 
         def spread_gamma_beta():

@@ -26,7 +26,6 @@ NB = 512
 NC = E // NB
 NP = E // 512
 NV = 336
-FC = 320
 LAST_SPLIT = 352
 
 
@@ -213,11 +212,8 @@ def tile_selfattention_pa_kernel(tc, h_attn, x, out_w, ln_gamma, ln_beta, out_0,
             yc[i] = work.tile([P, E], F32, name="yc")
             ut[i] = work.tile([P, E], F32, name="ut", bufs=4)
             junk = work.tile([P, E], BF16, name="junk", bufs=2)
-            nc.scalar.activation(
-                out=yc[i][:, 0:FC], in_=yt[i][:, 0:FC], func=ACT.Identity, bias=negmean, scale=1.0
-            )
             nc.gpsimd.tensor_scalar(
-                out=yc[i][:, FC:E], in0=yt[i][:, FC:E], scalar1=negmean, scalar2=1.0, op0=ALU.add, op1=ALU.mult
+                out=yc[i][:], in0=yt[i][:], scalar1=negmean, scalar2=1.0, op0=ALU.add, op1=ALU.mult
             )
             nc.gpsimd.tensor_tensor(out=ut[i][:], in0=yc[i][:], in1=gt[:], op=ALU.mult)
             nc.scalar.activation(

@@ -103,13 +103,18 @@ def tile_selfattention_pa_kernel(tc, h_attn, x, out_w, ln_gamma, ln_beta, out_0,
 
         gt = const.tile([P, E], BF16, name="gt")
         bt = {}
+        for c in range(NC):
+            bt[c] = ps_c.tile([P, NB], F32, name="bt%d" % c)
+
+        def keep_warm(rows):
+            for c in range(NC):
+                nc.tensor.matmul(bt[c][:], lhsT=ones[:], rhs=rows, start=True, stop=True)
 
         def spread_gamma_beta():
             for c in range(NC):
                 gp = ps_xt.tile([P, NB], F32, name="gp", tag="xt")
                 nc.tensor.matmul(gp[:], lhsT=ones[:], rhs=crow[:, c * NB:(c + 1) * NB], start=True, stop=True)
                 nc.scalar.copy(out=gt[:, c * NB:(c + 1) * NB], in_=gp[:])
-                bt[c] = ps_c.tile([P, NB], F32, name="bt%d" % c)
                 nc.tensor.matmul(
                     bt[c][:], lhsT=ones[:], rhs=crow[:, E + c * NB:E + (c + 1) * NB], start=True, stop=True
                 )
@@ -279,16 +284,21 @@ def tile_selfattention_pa_kernel(tc, h_attn, x, out_w, ln_gamma, ln_beta, out_0,
                 nc.sync.dma_start(out=o1v[gi // QB, gi % QB], in_=o8[gi][:].bitcast(U8))
 
         w_interleave(0, 0)
+        keep_warm(wraw[0][:, 0, 0, :])
         w_interleave(0, 1)
+        keep_warm(wraw[0][:, 1, 0, :])
         front_pe(0)
         front_s(0)
+        keep_warm(xs[0][:, 0, 0:NB])
         w_quant(0, 0)
         w_quant(0, 1)
         quant(0)
+        keep_warm(wraw[1][:, 0, 0, :])
         mmc(0, 0)
         w_interleave(1, 0)
         p1c(0, 0)
         w_interleave(1, 1)
+        keep_warm(wraw[1][:, 1, 0, :])
         front_pe(1)
         front_s(1)
         front_pe(2)

@@ -102,13 +102,11 @@ def tile_selfattention_pa_kernel(tc, h_attn, x, out_w, ln_gamma, ln_beta, out_0,
         load_x(NT - 1)
 
         gt = const.tile([P, E], BF16, name="gt")
-        bt = {}
-        for c in range(NC):
-            bt[c] = ps_c.tile([P, NB], F32, name="bt%d" % c)
+        bt = ps_c.tile([P, E], BF16, name="bt")
 
         def keep_warm(rows):
             for c in range(NC):
-                nc.tensor.matmul(bt[c][:], lhsT=ones[:], rhs=rows, start=True, stop=True)
+                nc.tensor.matmul(bt[:, c * NB:(c + 1) * NB], lhsT=ones[:], rhs=rows, start=True, stop=True)
 
         def spread_gamma_beta():
             for c in range(NC):
@@ -116,7 +114,11 @@ def tile_selfattention_pa_kernel(tc, h_attn, x, out_w, ln_gamma, ln_beta, out_0,
                 nc.tensor.matmul(gp[:], lhsT=ones[:], rhs=crow[:, c * NB:(c + 1) * NB], start=True, stop=True)
                 nc.scalar.copy(out=gt[:, c * NB:(c + 1) * NB], in_=gp[:])
                 nc.tensor.matmul(
-                    bt[c][:], lhsT=ones[:], rhs=crow[:, E + c * NB:E + (c + 1) * NB], start=True, stop=True
+                    bt[:, c * NB:(c + 1) * NB],
+                    lhsT=ones[:],
+                    rhs=crow[:, E + c * NB:E + (c + 1) * NB],
+                    start=True,
+                    stop=True,
                 )
 
         wgr = {}
@@ -235,15 +237,14 @@ def tile_selfattention_pa_kernel(tc, h_attn, x, out_w, ln_gamma, ln_beta, out_0,
         def fin(i):
             gi, j = divmod(i, J)
             ot[i] = outp.tile([P, E], F32, name="ot")
-            for c in range(NC):
-                nc.vector.scalar_tensor_tensor(
-                    out=ot[i][:, c * NB:(c + 1) * NB],
-                    in0=ut[i][:, c * NB:(c + 1) * NB],
-                    scalar=sst[gi][:, 2 + j:3 + j],
-                    in1=bt[c][:],
-                    op0=ALU.mult,
-                    op1=ALU.add,
-                )
+            nc.vector.scalar_tensor_tensor(
+                out=ot[i][:],
+                in0=ut[i][:],
+                scalar=sst[gi][:, 2 + j:3 + j],
+                in1=bt[:],
+                op0=ALU.mult,
+                op1=ALU.add,
+            )
             nc.sync.dma_start(out=o0v[gi // QB, gi % QB, j], in_=ot[i][:])
 
         def amax(i):

@@ -44,7 +44,7 @@ def tile_selfattention_pa_kernel(tc, h_attn, x, out_w, ln_gamma, ln_beta, out_0,
         mxp = ctx.enter_context(tc.tile_pool(name="mxp", bufs=3))
         work = ctx.enter_context(tc.tile_pool(name="work", bufs=3))
         outp = ctx.enter_context(tc.tile_pool(name="outp", bufs=7))
-        stat = ctx.enter_context(tc.tile_pool(name="stat", bufs=4))
+        stat = ctx.enter_context(tc.tile_pool(name="stat", bufs=5))
         ps_acc = ctx.enter_context(tc.psum_pool(name="ps_acc", bufs=4))
         ps_xt = ctx.enter_context(tc.psum_pool(name="ps_xt", bufs=2))
         ps_c = ctx.enter_context(tc.psum_pool(name="ps_c", bufs=1))
@@ -218,14 +218,25 @@ def tile_selfattention_pa_kernel(tc, h_attn, x, out_w, ln_gamma, ln_beta, out_0,
             )
             yc[i] = work.tile([P, E], F32, name="yc")
             ut[i] = work.tile([P, E], F32, name="ut", bufs=4)
-            junk = work.tile([P, E], BF16, name="junk", bufs=2)
             nc.gpsimd.tensor_scalar(
                 out=yc[i][:], in0=yt[i][:], scalar1=negmean, scalar2=1.0, op0=ALU.add, op1=ALU.mult
             )
             nc.gpsimd.tensor_tensor(out=ut[i][:], in0=yc[i][:], in1=gt[:], op=ALU.mult)
+
+        def squares(i):
+            gi, j = divmod(i, J)
+            junk = work.tile([P, E], BF16, name="junk", bufs=2)
             nc.scalar.activation(
-                out=junk[:], in_=yt[i][:], func=ACT.Square, bias=negmean, scale=1.0, accum_out=sst[gi][:, j:j + 1]
+                out=junk[:],
+                in_=yt[i][:],
+                func=ACT.Square,
+                bias=sst[gi][:, 6 + j:7 + j],
+                scale=1.0,
+                accum_out=sst[gi][:, j:j + 1],
             )
+
+        def rstd(i):
+            gi, j = divmod(i, J)
             nc.scalar.activation(
                 out=sst[gi][:, 2 + j:3 + j],
                 in_=sst[gi][:, j:j + 1],
@@ -309,6 +320,7 @@ def tile_selfattention_pa_kernel(tc, h_attn, x, out_w, ln_gamma, ln_beta, out_0,
         w_quant(1, 1)
         mmc(0, 1)
         quant(1)
+        due = []
         for t in range(NT + 3):
             if t + 1 < NT:
                 mmc(t + 1, 0)
@@ -330,15 +342,24 @@ def tile_selfattention_pa_kernel(tc, h_attn, x, out_w, ln_gamma, ln_beta, out_0,
                 recip(NG - 1, (t - 3) % J, (t - 3) % J + 1)
             if t < NT:
                 mid(t)
+                if due:
+                    cast(due[0][0], due[0][1], E)
+                    due.remove(due[0])
+                squares(t)
             if t + 3 < NT:
                 front_s(t + 3)
+            if t < NT:
+                rstd(t)
             if 0 <= t - 2 < NT:
                 fin(t - 2)
             if full:
                 factor((t - 5) // J, 0, J)
-                cast((t - 5) // J, 0, E)
-            if t >= 6 and (t - 6) % J == 0 and (t - 6) // J <= NG - 3:
-                cast((t - 6) // J, 1, E)
+                due.extend([((t - 5) // J, 0), ((t - 5) // J, 1)])
+            if t >= NT - 1 and due and due[0][0] <= NG - 3:
+                cast(due[0][0], due[0][1], E)
+                due.remove(due[0])
+            if t == NT + 1:
+                cast(NG - 2, 0, E)
             if t == NT + 1:
                 cast(NG - 2, 1, E)
             if t - 3 >= NT - J:

@@ -27,6 +27,7 @@ NC = E // NB
 NP = E // 512
 NV = 336
 LAST_SPLIT = 352
+FC = 192
 
 
 def tile_selfattention_pa_kernel(tc, h_attn, x, out_w, ln_gamma, ln_beta, out_0, out_1):
@@ -219,7 +220,13 @@ def tile_selfattention_pa_kernel(tc, h_attn, x, out_w, ln_gamma, ln_beta, out_0,
             yc[i] = work.tile([P, E], F32, name="yc")
             ut[i] = work.tile([P, E], F32, name="ut", bufs=4)
             nc.gpsimd.tensor_scalar(
-                out=yc[i][:], in0=yt[i][:], scalar1=negmean, scalar2=1.0, op0=ALU.add, op1=ALU.mult
+                out=yc[i][:, FC:E], in0=yt[i][:, FC:E], scalar1=negmean, scalar2=1.0, op0=ALU.add, op1=ALU.mult
+            )
+
+        def centre_s(i):
+            gi, j = divmod(i, J)
+            nc.scalar.activation(
+                out=yc[i][:, 0:FC], in_=yt[i][:, 0:FC], func=ACT.Identity, bias=sst[gi][:, 6 + j:7 + j], scale=1.0
             )
             nc.gpsimd.tensor_tensor(out=ut[i][:], in0=yc[i][:], in1=gt[:], op=ALU.mult)
 
@@ -345,6 +352,7 @@ def tile_selfattention_pa_kernel(tc, h_attn, x, out_w, ln_gamma, ln_beta, out_0,
                 if due:
                     cast(due[0][0], due[0][1], E)
                     due.remove(due[0])
+                centre_s(t)
                 squares(t)
             if t + 3 < NT:
                 front_s(t + 3)

@@ -27,7 +27,7 @@ NC = E // NB
 NP = E // 512
 NV = 336
 LAST_SPLIT = 352
-FC = 192
+FC = 224
 
 
 def tile_selfattention_pa_kernel(tc, h_attn, x, out_w, ln_gamma, ln_beta, out_0, out_1):

from contextlib import ExitStack

import concourse.mybir as mybir
from concourse.masks import make_identity

B, H, S, D = 2, 4, 1024, 256
E = H * D
LN_EPS = 1e-6
FLOPS = 2 * B * S * E * E

F32 = mybir.dt.float32
BF16 = mybir.dt.bfloat16
U32 = mybir.dt.uint32
U8 = mybir.dt.uint8
FP8X4 = mybir.dt.float8_e4m3fn_x4
FP8 = mybir.dt.float8_e4m3fn
ALU = mybir.AluOpType
ACT = mybir.ActivationFunctionType
AX = mybir.AxisListType

P = 128
J = 2
NG = B * S // (P * J)
NT = NG * J
NB = 512
NC = E // NB
NP = E // 512
NV = 336
LAST_SPLIT = 352
FC = 224


def tile_selfattention_pa_kernel(tc, h_attn, x, out_w, ln_gamma, ln_beta, out_0, out_1):
    nc = tc.nc
    hv = h_attn.rearrange("b h (q p j) d -> b q j p h d", p=P, j=J)
    xv = x.rearrange("b (q p j) n -> b q j p n", p=P, j=J)
    o0v = out_0.rearrange("b (q p j) n -> b q j p n", p=P, j=J)
    o1v = out_1.rearrange("b (q p j) n -> b q p j n", p=P, j=J)
    wv = out_w.rearrange("(g p t) n -> g p t n", p=P, t=4)
    QB = NG // B

    with ExitStack() as ctx:
        const = ctx.enter_context(tc.tile_pool(name="const", bufs=1))
        inp = ctx.enter_context(tc.tile_pool(name="inp", bufs=1))
        mxp = ctx.enter_context(tc.tile_pool(name="mxp", bufs=3))
        work = ctx.enter_context(tc.tile_pool(name="work", bufs=3))
        outp = ctx.enter_context(tc.tile_pool(name="outp", bufs=7))
        stat = ctx.enter_context(tc.tile_pool(name="stat", bufs=5))
        ps_acc = ctx.enter_context(tc.psum_pool(name="ps_acc", bufs=4))
        ps_xt = ctx.enter_context(tc.psum_pool(name="ps_xt", bufs=2))
        ps_c = ctx.enter_context(tc.psum_pool(name="ps_c", bufs=1))
        ctx.enter_context(tc.manual_schedule())

        ident = const.tile([P, P], F32, name="ident")
        make_identity(nc, ident[:])
        crow = const.tile([P, 2 * E], BF16, name="crow")
        nc.vector.memset(crow[:], 0.0)
        eps_t = const.tile([P, 1], F32, name="eps_t")
        nc.vector.memset(eps_t[:], LN_EPS)
        zero_t = const.tile([P, 1], F32, name="zero_t")
        nc.vector.memset(zero_t[:], 0.0)
        ones = const.tile([P, P], BF16, name="ones")
        nc.vector.memset(ones[:], 1.0)
        warm = const.tile([P, 1], F32, name="warm")
        nc.scalar.dma_start(out=crow[0:1, 0:E], in_=ln_gamma.rearrange("(o n) -> o n", o=1))
        nc.scalar.dma_start(out=crow[0:1, E:2 * E], in_=ln_beta.rearrange("(o n) -> o n", o=1))
        nc.scalar.activation(out=warm[:], in_=eps_t[:], func=ACT.Abs_reciprocal_sqrt)

        hs = {}
        xs = {}
        wraw = {}

        def load_h(i):
            gi, j = divmod(i, J)
            if j == 0:
                hs[gi] = inp.tile([P, J, E], BF16, name="hs%d" % gi)
            nc.sync.dma_start(
                out=hs[gi][:, j, :].rearrange("p (h d) -> p h d", h=H),
                in_=hv[gi // QB, gi % QB, j],
            )

        def load_x(i):
            gi, j = divmod(i, J)
            if j == 0:
                xs[gi] = inp.tile([P, J, E], BF16, name="xs%d" % gi)
            nc.sync.dma_start(out=xs[gi][:, j, :], in_=xv[gi // QB, gi % QB, j])

        def load_w(c, g):
            if g == 0:
                wraw[c] = inp.tile([P, NP, 4, NB], BF16, name="wraw%d" % c)
            nc.sync.dma_start(out=wraw[c][:, g, :, :], in_=wv[g, :, :, c * NB:(c + 1) * NB])

        load_w(0, 0)
        load_w(0, 1)
        load_h(0)
        load_x(0)
        load_w(1, 0)
        load_w(1, 1)
        load_h(1)
        for i in range(2, NT):
            load_h(i)
            load_x(i - 1)
        load_x(NT - 1)

        gt = const.tile([P, E], BF16, name="gt")
        bt = ps_c.tile([P, E], BF16, name="bt")

        def keep_warm(rows):
            for c in range(NC):
                nc.tensor.matmul(bt[:, c * NB:(c + 1) * NB], lhsT=ones[:], rhs=rows, start=True, stop=True)

        def spread_gamma_beta():
            for c in range(NC):
                gp = ps_xt.tile([P, NB], F32, name="gp", tag="xt")
                nc.tensor.matmul(gp[:], lhsT=ones[:], rhs=crow[:, c * NB:(c + 1) * NB], start=True, stop=True)
                nc.scalar.copy(out=gt[:, c * NB:(c + 1) * NB], in_=gp[:])
                nc.tensor.matmul(
                    bt[:, c * NB:(c + 1) * NB],
                    lhsT=ones[:],
                    rhs=crow[:, E + c * NB:E + (c + 1) * NB],
                    start=True,
                    stop=True,
                )

        wgr = {}
        wc = {}
        ws = {}

        def w_interleave(c, g):
            if g == 0:
                wgr[c] = inp.tile([P, NP, NB, 4], BF16, name="wgr%d" % c, align_bytes=64)
            nc.vector.tensor_copy(out=wgr[c][:, g, 0:NV, :], in_=wraw[c][:, g, :, 0:NV].rearrange("p t n -> p n t"))
            nc.scalar.copy(out=wgr[c][:, g, NV:NB, :], in_=wraw[c][:, g, :, NV:NB].rearrange("p t n -> p n t"))

        def w_quant(c, g):
            if g == 0:
                wc[c] = inp.tile([P, NP, NB], U32, name="wc%d" % c, align_bytes=64)
                ws[c] = inp.tile([P, NP, NB], U8, name="ws%d" % c, align_bytes=64)
            nc.vector.quantize_mx(
                out=wc[c][:, g, :].bitcast(FP8X4),
                scales=ws[c][:, g, :],
                in_=wgr[c][:, g, :, :].rearrange("p n t -> p (n t)"),
            )

        mg = {}
        mc = {}
        ms = {}
        acc = {}
        yt = {}
        yc = {}
        ut = {}
        ot = {}
        o8 = {}
        vst = {}
        sst = {}

        xts = {}

        def front_pe(i):
            gi, j = divmod(i, J)
            words = hs[gi][:, j, :].bitcast(F32)
            xts[i] = ps_xt.tile([P, NP, 2, P], F32, name="xt", tag="xt")
            for g in range(NP):
                for u in range(2):
                    nc.tensor.transpose(xts[i][:, g, u, :], words[:, 256 * g + u:256 * (g + 1):2], ident[:])

        def front_s(i):
            mg[i] = mxp.tile([P, NP, P, 4], BF16, name="mg", align_bytes=64)
            nc.scalar.copy(out=mg[i][:].bitcast(F32), in_=xts[i][:].rearrange("p g u r -> p g r u"))

        def quant(i):
            mc[i] = mxp.tile([P, NP * P], U32, name="mc", align_bytes=64)
            ms[i] = mxp.tile([P, NP * P], U8, name="ms", align_bytes=64)
            nc.vector.quantize_mx(
                out=mc[i][:].bitcast(FP8X4),
                scales=ms[i][:],
                in_=mg[i][:].rearrange("p g r t -> p (g r t)"),
            )

        def mmc(i, c):
            acc[i, c] = ps_acc.tile([P, NB], F32, name="acc")
            for g in range(NP):
                nc.tensor.matmul_mx(
                    out=acc[i, c][:],
                    lhsT=mc[i][:, g * P:(g + 1) * P].bitcast(FP8X4),
                    lhsT_scale=ms[i][:, g * P:(g + 1) * P],
                    rhs=wc[c][:, g, :].bitcast(FP8X4),
                    rhs_scale=ws[c][:, g, :],
                    start=(g == 0),
                    stop=(g == NP - 1),
                )

        def p1c(i, c):
            gi, j = divmod(i, J)
            if c == 0:
                if j == 0:
                    vst[gi] = stat.tile([P, 8], F32, name="vst")
                    sst[gi] = stat.tile([P, 16], F32, name="sst")
                yt[i] = work.tile([P, E], F32, name="yt")
            nc.vector.scalar_tensor_tensor(
                out=yt[i][:, c * NB:(c + 1) * NB],
                in0=xs[gi][:, j, c * NB:(c + 1) * NB],
                scalar=1.0,
                in1=acc[i, c][:],
                op0=ALU.mult,
                op1=ALU.add,
                accum_out=vst[gi][:, 2 * j + c:2 * j + c + 1],
            )

        def mid(i):
            gi, j = divmod(i, J)
            negmean = sst[gi][:, 6 + j:7 + j]
            nc.scalar.activation(
                out=sst[gi][:, 8 + 2 * j:10 + 2 * j],
                in_=vst[gi][:, 2 * j:2 * j + 2],
                func=ACT.Copy,
                scale=-1.0 / E,
                accum_out=negmean,
            )
            yc[i] = work.tile([P, E], F32, name="yc")
            ut[i] = work.tile([P, E], F32, name="ut", bufs=4)
            nc.gpsimd.tensor_scalar(
                out=yc[i][:, FC:E], in0=yt[i][:, FC:E], scalar1=negmean, scalar2=1.0, op0=ALU.add, op1=ALU.mult
            )

        def centre_s(i):
            gi, j = divmod(i, J)
            nc.scalar.activation(
                out=yc[i][:, 0:FC], in_=yt[i][:, 0:FC], func=ACT.Identity, bias=sst[gi][:, 6 + j:7 + j], scale=1.0
            )
            nc.gpsimd.tensor_tensor(out=ut[i][:], in0=yc[i][:], in1=gt[:], op=ALU.mult)

        def squares(i):
            gi, j = divmod(i, J)
            junk = work.tile([P, E], BF16, name="junk", bufs=2)
            nc.scalar.activation(
                out=junk[:],
                in_=yt[i][:],
                func=ACT.Square,
                bias=sst[gi][:, 6 + j:7 + j],
                scale=1.0,
                accum_out=sst[gi][:, j:j + 1],
            )

        def rstd(i):
            gi, j = divmod(i, J)
            nc.scalar.activation(
                out=sst[gi][:, 2 + j:3 + j],
                in_=sst[gi][:, j:j + 1],
                func=ACT.Abs_reciprocal_sqrt,
                bias=eps_t[:, 0:1],
                scale=1.0 / E,
            )

        def fin(i):
            gi, j = divmod(i, J)
            ot[i] = outp.tile([P, E], F32, name="ot")
            nc.vector.scalar_tensor_tensor(
                out=ot[i][:],
                in0=ut[i][:],
                scalar=sst[gi][:, 2 + j:3 + j],
                in1=bt[:],
                op0=ALU.mult,
                op1=ALU.add,
            )
            nc.sync.dma_start(out=o0v[gi // QB, gi % QB, j], in_=ot[i][:])

        def amax(i):
            gi, j = divmod(i, J)
            nc.vector.tensor_reduce(
                out=vst[gi][:, 4 + j:5 + j], in_=ot[i][:], axis=AX.X, op=ALU.max, apply_absolute_value=True
            )

        def recip(gi, j0, j1):
            nc.vector.reciprocal(out=vst[gi][:, 6 + j0:6 + j1], in_=vst[gi][:, 4 + j0:4 + j1])

        def factor(gi, j0, j1):
            nc.scalar.activation(
                out=sst[gi][:, 4 + j0:4 + j1], in_=vst[gi][:, 6 + j0:6 + j1], func=ACT.Copy, scale=448.0
            )

        def cast(gi, j, split):
            if j == 0:
                o8[gi] = outp.tile([P, J, E], FP8, name="o8", bufs=3)
            nc.scalar.activation(
                out=o8[gi][:, j, 0:split],
                in_=ot[gi * J + j][:, 0:split],
                func=ACT.Identity,
                scale=sst[gi][:, 4 + j:5 + j],
                bias=zero_t[:, 0:1],
                saturate=False,
            )
            if split < E:
                nc.vector.tensor_scalar(
                    out=o8[gi][:, j, split:E],
                    in0=ot[gi * J + j][:, split:E],
                    scalar1=sst[gi][:, 4 + j:5 + j],
                    scalar2=None,
                    op0=ALU.mult,
                    saturate=False,
                )
            if j == J - 1:
                nc.sync.dma_start(out=o1v[gi // QB, gi % QB], in_=o8[gi][:].bitcast(U8))

        w_interleave(0, 0)
        keep_warm(wraw[0][:, 0, 0, :])
        w_interleave(0, 1)
        keep_warm(wraw[0][:, 1, 0, :])
        front_pe(0)
        front_s(0)
        keep_warm(xs[0][:, 0, 0:NB])
        w_quant(0, 0)
        w_quant(0, 1)
        quant(0)
        keep_warm(wraw[1][:, 0, 0, :])
        mmc(0, 0)
        w_interleave(1, 0)
        p1c(0, 0)
        w_interleave(1, 1)
        keep_warm(wraw[1][:, 1, 0, :])
        front_pe(1)
        front_s(1)
        front_pe(2)
        front_s(2)
        spread_gamma_beta()
        w_quant(1, 0)
        w_quant(1, 1)
        mmc(0, 1)
        quant(1)
        due = []
        for t in range(NT + 3):
            if t + 1 < NT:
                mmc(t + 1, 0)
                mmc(t + 1, 1)
            if t + 3 < NT:
                front_pe(t + 3)
            if t < NT:
                if t > 0:
                    p1c(t, 0)
                p1c(t, 1)
            full = t >= 5 and (t - 5) % J == 0 and (t - 5) // J <= NG - 2
            if full:
                recip((t - 5) // J, 0, J)
            if t + 2 < NT:
                quant(t + 2)
            if 0 <= t - 3 < NT:
                amax(t - 3)
            if t - 3 >= NT - J:
                recip(NG - 1, (t - 3) % J, (t - 3) % J + 1)
            if t < NT:
                mid(t)
                if due:
                    cast(due[0][0], due[0][1], E)
                    due.remove(due[0])
                centre_s(t)
                squares(t)
            if t + 3 < NT:
                front_s(t + 3)
            if t < NT:
                rstd(t)
            if 0 <= t - 2 < NT:
                fin(t - 2)
            if full:
                factor((t - 5) // J, 0, J)
                due.extend([((t - 5) // J, 0), ((t - 5) // J, 1)])
            if t >= NT - 1 and due and due[0][0] <= NG - 3:
                cast(due[0][0], due[0][1], E)
                due.remove(due[0])
            if t == NT + 1:
                cast(NG - 2, 0, E)
            if t == NT + 1:
                cast(NG - 2, 1, E)
            if t - 3 >= NT - J:
                factor(NG - 1, (t - 3) % J, (t - 3) % J + 1)
                cast(NG - 1, (t - 3) % J, E if t - 3 < NT - 1 else LAST_SPLIT)
